import numpy as np
import ml_dtypes

BF16 = ml_dtypes.bfloat16


def bf(x):
    return np.asarray(x, np.float32).astype(BF16)


def f32(x):
    return np.asarray(x, np.float32)


def f64(x):
    return np.asarray(x).astype(np.float64)


def striped(idx):
    return np.tile(idx.reshape(-1, 16).T, (8, 1))


H, C, S, B, N = 128, 640, 512, 128, 384


def sigmoid(v):
    return 1.0 / (1.0 + np.exp(-v))


def setup_inputs():
    return {"table": f32(np.random.standard_normal((C, S))), "ua": bf(3.0 * np.random.standard_normal((H, C)) / np.sqrt(H)), "ub": bf(3.0 * np.random.standard_normal((H, C)) / np.sqrt(H)), "b": f32(0.1 * np.random.standard_normal((C, 1))), "offs": striped(np.random.permutation(np.tile(np.arange(S), 2))[:N])}


def reference(table, ua, ub, b, offs):
    idx = offs[:16].T.reshape(-1)
    ia, ib, ir = idx.reshape(N // B, B)
    tab, bias = f64(table), f64(b)

    def leaf(ix):
        gi, gfa, gfb, go, gu = (tab[:, ix] + bias).reshape(C // H, H, B)
        cl = sigmoid(gi) * np.tanh(gu)
        return sigmoid(go) * np.tanh(cl), cl

    ha, ca = leaf(ia)
    hb, cb = leaf(ib)
    kids = bias + f64(ua).T @ ha + f64(ub).T @ hb
    gi, gfa, gfb, go, gu = (tab[:, ir] + kids).reshape(C // H, H, B)
    cr = sigmoid(gi) * np.tanh(gu) + sigmoid(gfa) * ca + sigmoid(gfb) * cb
    return sigmoid(go) * np.tanh(cr)

@@ -1,0 +1,98 @@
+import concourse.mybir as mybir
+
+F32 = mybir.dt.float32
+BF16 = mybir.dt.bfloat16
+U16 = mybir.dt.uint16
+ADD = mybir.AluOpType.add
+MULT = mybir.AluOpType.mult
+SIGMOID = mybir.ActivationFunctionType.Sigmoid
+TANH = mybir.ActivationFunctionType.Tanh
+IDENTITY = mybir.ActivationFunctionType.Identity
+
+H = 128
+S = 512
+B = 128
+LEAVES = 2 * B
+N = LEAVES + B
+GATES = ("i", "fa", "fb", "o", "u")
+FUNC = {"i": SIGMOID, "fa": SIGMOID, "fb": SIGMOID, "o": SIGMOID, "u": TANH}
+
+FLOPS = 2 * 2 * H * len(GATES) * H * B
+
+
+def tile_sympleagent_kernel(tc, table, ua, ub, b, offs, out):
+    nc = tc.nc
+    with (
+        tc.tile_pool(name="held", bufs=1) as held,
+        tc.psum_pool(name="psum", bufs=1) as psum,
+    ):
+        offsets = held.tile([128, N // 16], U16, name="offsets")
+        nc.sync.dma_start(offsets[:], offs)
+
+        bias = held.tile([H, len(GATES)], F32, name="bias")
+        with nc.allow_non_contiguous_dma(reason="2.5 KiB of bias, one element to a partition"):
+            nc.scalar.dma_start(bias[:], b.rearrange("(g k) o -> k (g o)", k=H))
+
+        window = {}
+        for turn, gate in enumerate(("i", "u", "o", "fa", "fb")):
+            g = GATES.index(gate)
+            window[gate] = held.tile([H, S], F32, name="window_" + gate)
+            queue = nc.sync if turn % 2 == 0 else nc.scalar
+            queue.dma_start(window[gate][:], table[g * H : (g + 1) * H, :])
+
+        ua_sb = held.tile([H, len(GATES) * H], BF16, name="ua_sb")
+        ub_sb = held.tile([H, len(GATES) * H], BF16, name="ub_sb")
+        nc.gpsimd.dma_start(ua_sb[:], ua)
+        nc.gpsimd.dma_start(ub_sb[:], ub)
+
+        def bias_of(gate):
+            g = GATES.index(gate)
+            return bias[:, g : g + 1]
+
+        bias_wide = {}
+        for gate in ("i", "u", "o"):
+            bias_wide[gate] = held.tile([H, LEAVES], F32, name="bias_wide_" + gate)
+            nc.vector.tensor_copy(bias_wide[gate][:], bias_of(gate).to_broadcast([H, LEAVES]))
+
+        leaf_offsets = offsets[:, 0 : LEAVES // 16]
+        leaf = {}
+        for gate in ("i", "u", "o"):
+            z = held.tile([H, LEAVES], F32, name="z_leaf_" + gate)
+            nc.vector.tensor_tensor(z[:], window[gate][:].indirect(leaf_offsets), bias_wide[gate][:], ADD)
+            leaf[gate] = held.tile([H, LEAVES], F32, name="leaf_" + gate)
+            nc.scalar.activation(leaf[gate][:], z[:], FUNC[gate])
+
+        cl = held.tile([H, LEAVES], F32, name="cl")
+        nc.vector.tensor_tensor(cl[:], leaf["i"][:], leaf["u"][:], MULT)
+        tanh_cl = held.tile([H, LEAVES], F32, name="tanh_cl")
+        nc.scalar.activation(tanh_cl[:], cl[:], TANH)
+        hl = held.tile([H, LEAVES], BF16, name="hl")
+        nc.vector.tensor_tensor(hl[:], leaf["o"][:], tanh_cl[:], MULT)
+
+        root_offsets = offsets[:, LEAVES // 16 : N // 16]
+        root = {}
+        for gate in ("i", "u", "fa", "fb", "o"):
+            g = GATES.index(gate)
+            products = psum.tile([H, B], F32, name="products_" + gate)
+            nc.tensor.matmul(products[:], ua_sb[:, g * H : (g + 1) * H], hl[:, 0:B], start=True, stop=False)
+            nc.tensor.matmul(products[:], ub_sb[:, g * H : (g + 1) * H], hl[:, B:LEAVES], start=False, stop=True)
+            kids = held.tile([H, B], F32, name="kids_" + gate)
+            nc.scalar.activation(kids[:], products[:], IDENTITY, bias=bias_of(gate))
+            z = held.tile([H, B], F32, name="z_root_" + gate)
+            nc.vector.tensor_tensor(z[:], window[gate][:].indirect(root_offsets), kids[:], ADD)
+            root[gate] = held.tile([H, B], F32, name="root_" + gate)
+            nc.scalar.activation(root[gate][:], z[:], FUNC[gate])
+
+        cr = held.tile([H, B], F32, name="cr")
+        from_left = held.tile([H, B], F32, name="from_left")
+        from_right = held.tile([H, B], F32, name="from_right")
+        nc.vector.tensor_tensor(cr[:], root["i"][:], root["u"][:], MULT)
+        nc.vector.tensor_tensor(from_left[:], root["fa"][:], cl[:, 0:B], MULT)
+        nc.vector.tensor_tensor(from_right[:], root["fb"][:], cl[:, B:LEAVES], MULT)
+        nc.vector.tensor_tensor(cr[:], cr[:], from_left[:], ADD)
+        nc.vector.tensor_tensor(cr[:], cr[:], from_right[:], ADD)
+        tanh_cr = held.tile([H, B], F32, name="tanh_cr")
+        nc.scalar.activation(tanh_cr[:], cr[:], TANH)
+        hr = held.tile([H, B], F32, name="hr")
+        nc.vector.tensor_tensor(hr[:], root["o"][:], tanh_cr[:], MULT)
+        nc.sync.dma_start(out, hr[:])

@@ -34,16 +34,20 @@ def tile_sympleagent_kernel(tc, table, ua, ub, b, offs, out):
             nc.scalar.dma_start(bias[:], b.rearrange("(g k) o -> k (g o)", k=H))
 
         window = {}
-        for turn, gate in enumerate(("i", "u", "o", "fa", "fb")):
+
+        def load_window(gate):
             g = GATES.index(gate)
             window[gate] = held.tile([H, S], F32, name="window_" + gate)
-            queue = nc.sync if turn % 2 == 0 else nc.scalar
-            queue.dma_start(window[gate][:], table[g * H : (g + 1) * H, :])
+            nc.sync.dma_start(window[gate][:], table[g * H : (g + 1) * H, :])
 
+        for gate in ("i", "u", "o"):
+            load_window(gate)
         ua_sb = held.tile([H, len(GATES) * H], BF16, name="ua_sb")
         ub_sb = held.tile([H, len(GATES) * H], BF16, name="ub_sb")
-        nc.gpsimd.dma_start(ua_sb[:], ua)
-        nc.gpsimd.dma_start(ub_sb[:], ub)
+        nc.sync.dma_start(ua_sb[:], ua)
+        nc.sync.dma_start(ub_sb[:], ub)
+        for gate in ("fa", "fb"):
+            load_window(gate)
 
         def bias_of(gate):
             g = GATES.index(gate)

@@ -12,10 +12,12 @@ IDENTITY = mybir.ActivationFunctionType.Identity
 H = 128
 S = 512
 B = 128
-LEAVES = 2 * B
-N = LEAVES + B
+N = 3 * B
+PIECE = B // 16
 GATES = ("i", "fa", "fb", "o", "u")
 FUNC = {"i": SIGMOID, "fa": SIGMOID, "fb": SIGMOID, "o": SIGMOID, "u": TANH}
+SIDES = (0, 1)
+ROOTS = 2
 
 FLOPS = 2 * 2 * H * len(GATES) * H * B
 
@@ -42,10 +44,10 @@ def tile_sympleagent_kernel(tc, table, ua, ub, b, offs, out):
 
         for gate in ("i", "u", "o"):
             load_window(gate)
-        ua_sb = held.tile([H, len(GATES) * H], BF16, name="ua_sb")
-        ub_sb = held.tile([H, len(GATES) * H], BF16, name="ub_sb")
-        nc.sync.dma_start(ua_sb[:], ua)
-        nc.sync.dma_start(ub_sb[:], ub)
+        weights = []
+        for side, u_side in zip(SIDES, (ua, ub)):
+            weights.append(held.tile([H, len(GATES) * H], BF16, name="weights_" + str(side)))
+            nc.sync.dma_start(weights[side][:], u_side)
         for gate in ("fa", "fb"):
             load_window(gate)
 
@@ -53,46 +55,60 @@ def tile_sympleagent_kernel(tc, table, ua, ub, b, offs, out):
             g = GATES.index(gate)
             return bias[:, g : g + 1]
 
+        def look_up(gate, piece, other, name):
+            z = held.tile([H, B], F32, name="z_" + name)
+            picked = window[gate][:].indirect(offsets[:, piece * PIECE : (piece + 1) * PIECE])
+            nc.vector.tensor_tensor(z[:], picked, other[:], ADD)
+            gate_value = held.tile([H, B], F32, name="gate_" + name)
+            nc.scalar.activation(gate_value[:], z[:], FUNC[gate])
+            return gate_value
+
         bias_wide = {}
         for gate in ("i", "u", "o"):
-            bias_wide[gate] = held.tile([H, LEAVES], F32, name="bias_wide_" + gate)
-            nc.vector.tensor_copy(bias_wide[gate][:], bias_of(gate).to_broadcast([H, LEAVES]))
+            bias_wide[gate] = held.tile([H, B], F32, name="bias_wide_" + gate)
+            nc.vector.tensor_copy(bias_wide[gate][:], bias_of(gate).to_broadcast([H, B]))
 
-        leaf_offsets = offsets[:, 0 : LEAVES // 16]
         leaf = {}
         for gate in ("i", "u", "o"):
-            z = held.tile([H, LEAVES], F32, name="z_leaf_" + gate)
-            nc.vector.tensor_tensor(z[:], window[gate][:].indirect(leaf_offsets), bias_wide[gate][:], ADD)
-            leaf[gate] = held.tile([H, LEAVES], F32, name="leaf_" + gate)
-            nc.scalar.activation(leaf[gate][:], z[:], FUNC[gate])
+            for side in SIDES:
+                leaf[gate, side] = look_up(gate, side, bias_wide[gate], "leaf_" + gate + str(side))
 
-        cl = held.tile([H, LEAVES], F32, name="cl")
-        nc.vector.tensor_tensor(cl[:], leaf["i"][:], leaf["u"][:], MULT)
-        tanh_cl = held.tile([H, LEAVES], F32, name="tanh_cl")
-        nc.scalar.activation(tanh_cl[:], cl[:], TANH)
-        hl = held.tile([H, LEAVES], BF16, name="hl")
-        nc.vector.tensor_tensor(hl[:], leaf["o"][:], tanh_cl[:], MULT)
+        cl = []
+        tanh_cl = []
+        for side in SIDES:
+            cl.append(held.tile([H, B], F32, name="cl_" + str(side)))
+            nc.vector.tensor_tensor(cl[side][:], leaf["i", side][:], leaf["u", side][:], MULT)
+            tanh_cl.append(held.tile([H, B], F32, name="tanh_cl_" + str(side)))
+            nc.scalar.activation(tanh_cl[side][:], cl[side][:], TANH)
 
-        root_offsets = offsets[:, LEAVES // 16 : N // 16]
-        root = {}
-        for gate in ("i", "u", "fa", "fb", "o"):
-            g = GATES.index(gate)
-            products = psum.tile([H, B], F32, name="products_" + gate)
-            nc.tensor.matmul(products[:], ua_sb[:, g * H : (g + 1) * H], hl[:, 0:B], start=True, stop=False)
-            nc.tensor.matmul(products[:], ub_sb[:, g * H : (g + 1) * H], hl[:, B:LEAVES], start=False, stop=True)
-            kids = held.tile([H, B], F32, name="kids_" + gate)
-            nc.scalar.activation(kids[:], products[:], IDENTITY, bias=bias_of(gate))
-            z = held.tile([H, B], F32, name="z_root_" + gate)
-            nc.vector.tensor_tensor(z[:], window[gate][:].indirect(root_offsets), kids[:], ADD)
-            root[gate] = held.tile([H, B], F32, name="root_" + gate)
-            nc.scalar.activation(root[gate][:], z[:], FUNC[gate])
+        root_gates = ("i", "u", "fa", "fb", "o")
+        products = {gate: psum.tile([H, B], F32, name="products_" + gate) for gate in root_gates}
+        for side in SIDES:
+            hl = held.tile([H, B], BF16, name="hl_" + str(side))
+            nc.vector.tensor_tensor(hl[:], leaf["o", side][:], tanh_cl[side][:], MULT)
+            for gate in root_gates:
+                g = GATES.index(gate)
+                nc.tensor.matmul(
+                    products[gate][:],
+                    weights[side][:, g * H : (g + 1) * H],
+                    hl[:],
+                    start=(side == SIDES[0]),
+                    stop=(side == SIDES[-1]),
+                )
+
+        kids = {}
+        for gate in root_gates:
+            kids[gate] = held.tile([H, B], F32, name="kids_" + gate)
+            nc.scalar.activation(kids[gate][:], products[gate][:], IDENTITY, bias=bias_of(gate))
+
+        root = {gate: look_up(gate, ROOTS, kids[gate], "root_" + gate) for gate in root_gates}
 
         cr = held.tile([H, B], F32, name="cr")
         from_left = held.tile([H, B], F32, name="from_left")
         from_right = held.tile([H, B], F32, name="from_right")
         nc.vector.tensor_tensor(cr[:], root["i"][:], root["u"][:], MULT)
-        nc.vector.tensor_tensor(from_left[:], root["fa"][:], cl[:, 0:B], MULT)
-        nc.vector.tensor_tensor(from_right[:], root["fb"][:], cl[:, B:LEAVES], MULT)
+        nc.vector.tensor_tensor(from_left[:], root["fa"][:], cl[0][:], MULT)
+        nc.vector.tensor_tensor(from_right[:], root["fb"][:], cl[1][:], MULT)
         nc.vector.tensor_tensor(cr[:], cr[:], from_left[:], ADD)
         nc.vector.tensor_tensor(cr[:], cr[:], from_right[:], ADD)
         tanh_cr = held.tile([H, B], F32, name="tanh_cr")

@@ -12,12 +12,10 @@ IDENTITY = mybir.ActivationFunctionType.Identity
 H = 128
 S = 512
 B = 128
-N = 3 * B
-PIECE = B // 16
+LEAVES = 2 * B
+N = LEAVES + B
 GATES = ("i", "fa", "fb", "o", "u")
 FUNC = {"i": SIGMOID, "fa": SIGMOID, "fb": SIGMOID, "o": SIGMOID, "u": TANH}
-SIDES = (0, 1)
-ROOTS = 2
 
 FLOPS = 2 * 2 * H * len(GATES) * H * B
 
@@ -31,9 +29,8 @@ def tile_sympleagent_kernel(tc, table, ua, ub, b, offs, out):
         offsets = held.tile([128, N // 16], U16, name="offsets")
         nc.sync.dma_start(offsets[:], offs)
 
-        bias = held.tile([H, len(GATES)], F32, name="bias")
-        with nc.allow_non_contiguous_dma(reason="2.5 KiB of bias, one element to a partition"):
-            nc.scalar.dma_start(bias[:], b.rearrange("(g k) o -> k (g o)", k=H))
+        b_row = held.tile([1, len(GATES) * H], F32, name="b_row")
+        nc.scalar.dma_start(b_row[:], b.rearrange("c o -> o c"))
 
         window = {}
 
@@ -44,71 +41,65 @@ def tile_sympleagent_kernel(tc, table, ua, ub, b, offs, out):
 
         for gate in ("i", "u", "o"):
             load_window(gate)
-        weights = []
-        for side, u_side in zip(SIDES, (ua, ub)):
-            weights.append(held.tile([H, len(GATES) * H], BF16, name="weights_" + str(side)))
-            nc.sync.dma_start(weights[side][:], u_side)
+        ua_sb = held.tile([H, len(GATES) * H], BF16, name="ua_sb")
+        ub_sb = held.tile([H, len(GATES) * H], BF16, name="ub_sb")
+        nc.sync.dma_start(ua_sb[:], ua)
+        nc.sync.dma_start(ub_sb[:], ub)
         for gate in ("fa", "fb"):
             load_window(gate)
+
+        one = held.tile([1, 1], F32, name="one")
+        nc.vector.memset(one[:], 1.0)
+        bias_psum = psum.tile([H, len(GATES)], F32, name="bias_psum")
+        for g in range(len(GATES)):
+            nc.tensor.matmul(bias_psum[:, g : g + 1], b_row[:, g * H : (g + 1) * H], one[:], start=True, stop=True)
+        bias = held.tile([H, len(GATES)], F32, name="bias")
+        nc.vector.tensor_copy(bias[:], bias_psum[:])
 
         def bias_of(gate):
             g = GATES.index(gate)
             return bias[:, g : g + 1]
 
-        def look_up(gate, piece, other, name):
-            z = held.tile([H, B], F32, name="z_" + name)
-            picked = window[gate][:].indirect(offsets[:, piece * PIECE : (piece + 1) * PIECE])
-            nc.vector.tensor_tensor(z[:], picked, other[:], ADD)
-            gate_value = held.tile([H, B], F32, name="gate_" + name)
-            nc.scalar.activation(gate_value[:], z[:], FUNC[gate])
-            return gate_value
-
         bias_wide = {}
         for gate in ("i", "u", "o"):
-            bias_wide[gate] = held.tile([H, B], F32, name="bias_wide_" + gate)
-            nc.vector.tensor_copy(bias_wide[gate][:], bias_of(gate).to_broadcast([H, B]))
+            bias_wide[gate] = held.tile([H, LEAVES], F32, name="bias_wide_" + gate)
+            nc.vector.tensor_copy(bias_wide[gate][:], bias_of(gate).to_broadcast([H, LEAVES]))
 
+        leaf_offsets = offsets[:, 0 : LEAVES // 16]
         leaf = {}
         for gate in ("i", "u", "o"):
-            for side in SIDES:
-                leaf[gate, side] = look_up(gate, side, bias_wide[gate], "leaf_" + gate + str(side))
+            z = held.tile([H, LEAVES], F32, name="z_leaf_" + gate)
+            nc.vector.tensor_tensor(z[:], window[gate][:].indirect(leaf_offsets), bias_wide[gate][:], ADD)
+            leaf[gate] = held.tile([H, LEAVES], F32, name="leaf_" + gate)
+            nc.scalar.activation(leaf[gate][:], z[:], FUNC[gate])
 
-        cl = []
-        tanh_cl = []
-        for side in SIDES:
-            cl.append(held.tile([H, B], F32, name="cl_" + str(side)))
-            nc.vector.tensor_tensor(cl[side][:], leaf["i", side][:], leaf["u", side][:], MULT)
-            tanh_cl.append(held.tile([H, B], F32, name="tanh_cl_" + str(side)))
-            nc.scalar.activation(tanh_cl[side][:], cl[side][:], TANH)
+        cl = held.tile([H, LEAVES], F32, name="cl")
+        nc.vector.tensor_tensor(cl[:], leaf["i"][:], leaf["u"][:], MULT)
+        tanh_cl = held.tile([H, LEAVES], F32, name="tanh_cl")
+        nc.scalar.activation(tanh_cl[:], cl[:], TANH)
+        hl = held.tile([H, LEAVES], BF16, name="hl")
+        nc.vector.tensor_tensor(hl[:], leaf["o"][:], tanh_cl[:], MULT)
 
-        root_gates = ("i", "u", "fa", "fb", "o")
-        products = {gate: psum.tile([H, B], F32, name="products_" + gate) for gate in root_gates}
-        for side in SIDES:
-            hl = held.tile([H, B], BF16, name="hl_" + str(side))
-            nc.vector.tensor_tensor(hl[:], leaf["o", side][:], tanh_cl[side][:], MULT)
-            for gate in root_gates:
-                g = GATES.index(gate)
-                nc.tensor.matmul(
-                    products[gate][:],
-                    weights[side][:, g * H : (g + 1) * H],
-                    hl[:],
-                    start=(side == SIDES[0]),
-                    stop=(side == SIDES[-1]),
-                )
-
-        kids = {}
-        for gate in root_gates:
-            kids[gate] = held.tile([H, B], F32, name="kids_" + gate)
-            nc.scalar.activation(kids[gate][:], products[gate][:], IDENTITY, bias=bias_of(gate))
-
-        root = {gate: look_up(gate, ROOTS, kids[gate], "root_" + gate) for gate in root_gates}
+        root_offsets = offsets[:, LEAVES // 16 : N // 16]
+        root = {}
+        for gate in ("i", "u", "fa", "fb", "o"):
+            g = GATES.index(gate)
+            products = psum.tile([H, B], F32, name="products_" + gate)
+            nc.tensor.matmul(products[:], ua_sb[:, g * H : (g + 1) * H], hl[:, 0:B], start=True, stop=False)
+            nc.tensor.matmul(products[:], ub_sb[:, g * H : (g + 1) * H], hl[:, B:LEAVES], start=False, stop=True)
+            kids = held.tile([H, B], F32, name="kids_" + gate)
+            nc.scalar.activation(kids[:], products[:], IDENTITY, bias=bias_of(gate))
+            z = held.tile([H, B], F32, name="z_root_" + gate)
+            nc.vector.tensor_tensor(z[:], window[gate][:].indirect(root_offsets), kids[:], ADD)
+            root[gate] = held.tile([H, B], F32, name="root_" + gate)
+            nc.scalar.activation(root[gate][:], z[:], FUNC[gate])
 
         cr = held.tile([H, B], F32, name="cr")
         from_left = held.tile([H, B], F32, name="from_left")
         from_right = held.tile([H, B], F32, name="from_right")
         nc.vector.tensor_tensor(cr[:], root["i"][:], root["u"][:], MULT)
-        nc.vector.tensor_tensor(from_left[:], root["fa"][:], cl[0][:], MULT)
-        nc.vector.tensor_tensor(from_right[:], root["fb"][:], cl[1][:], MULT)
+        nc.vector.tensor_tensor(from_left[:], root["fa"][:], cl[:, 0:B], MULT)
+        nc.vector.tensor_tensor(from_right[:], root["fb"][:], cl[:, B:LEAVES], MULT)
         nc.vector.tensor_tensor(cr[:], cr[:], from_left[:], ADD)
         nc.vector.tensor_tensor(cr[:], cr[:], from_right[:], ADD)
         tanh_cr = held.tile([H, B], F32, name="tanh_cr")

@@ -1,3 +1,4 @@
+import concourse.masks as masks
 import concourse.mybir as mybir
 
 F32 = mybir.dt.float32
@@ -29,8 +30,8 @@ def tile_sympleagent_kernel(tc, table, ua, ub, b, offs, out):
         offsets = held.tile([128, N // 16], U16, name="offsets")
         nc.sync.dma_start(offsets[:], offs)
 
-        b_row = held.tile([1, len(GATES) * H], F32, name="b_row")
-        nc.scalar.dma_start(b_row[:], b.rearrange("c o -> o c"))
+        b_rows = held.tile([len(GATES), H], F32, name="b_rows")
+        nc.scalar.dma_start(b_rows[:], b.rearrange("(g k) o -> g (k o)", k=H))
 
         window = {}
 
@@ -48,22 +49,18 @@ def tile_sympleagent_kernel(tc, table, ua, ub, b, offs, out):
         for gate in ("fa", "fb"):
             load_window(gate)
 
-        one = held.tile([1, 1], F32, name="one")
-        nc.vector.memset(one[:], 1.0)
+        identity = held.tile([len(GATES), len(GATES)], F32, name="identity")
+        masks.make_identity(nc, identity[:])
         bias_psum = psum.tile([H, len(GATES)], F32, name="bias_psum")
-        for g in range(len(GATES)):
-            nc.tensor.matmul(bias_psum[:, g : g + 1], b_row[:, g * H : (g + 1) * H], one[:], start=True, stop=True)
-        bias = held.tile([H, len(GATES)], F32, name="bias")
-        nc.vector.tensor_copy(bias[:], bias_psum[:])
-
-        def bias_of(gate):
-            g = GATES.index(gate)
-            return bias[:, g : g + 1]
+        nc.tensor.matmul(bias_psum[:], b_rows[:], identity[:], start=True, stop=True)
 
         bias_wide = {}
         for gate in ("i", "u", "o"):
             bias_wide[gate] = held.tile([H, LEAVES], F32, name="bias_wide_" + gate)
-            nc.vector.tensor_copy(bias_wide[gate][:], bias_of(gate).to_broadcast([H, LEAVES]))
+            g = GATES.index(gate)
+            nc.vector.tensor_copy(bias_wide[gate][:], bias_psum[:, g : g + 1].to_broadcast([H, LEAVES]))
+        bias = held.tile([H, len(GATES)], F32, name="bias")
+        nc.vector.tensor_copy(bias[:], bias_psum[:])
 
         leaf_offsets = offsets[:, 0 : LEAVES // 16]
         leaf = {}
@@ -88,7 +85,7 @@ def tile_sympleagent_kernel(tc, table, ua, ub, b, offs, out):
             nc.tensor.matmul(products[:], ua_sb[:, g * H : (g + 1) * H], hl[:, 0:B], start=True, stop=False)
             nc.tensor.matmul(products[:], ub_sb[:, g * H : (g + 1) * H], hl[:, B:LEAVES], start=False, stop=True)
             kids = held.tile([H, B], F32, name="kids_" + gate)
-            nc.scalar.activation(kids[:], products[:], IDENTITY, bias=bias_of(gate))
+            nc.scalar.activation(kids[:], products[:], IDENTITY, bias=bias[:, g : g + 1])
             z = held.tile([H, B], F32, name="z_root_" + gate)
             nc.vector.tensor_tensor(z[:], window[gate][:].indirect(root_offsets), kids[:], ADD)
             root[gate] = held.tile([H, B], F32, name="root_" + gate)

@@ -1,4 +1,3 @@
-import concourse.masks as masks
 import concourse.mybir as mybir
 
 F32 = mybir.dt.float32
@@ -30,8 +29,9 @@ def tile_sympleagent_kernel(tc, table, ua, ub, b, offs, out):
         offsets = held.tile([128, N // 16], U16, name="offsets")
         nc.sync.dma_start(offsets[:], offs)
 
-        b_rows = held.tile([len(GATES), H], F32, name="b_rows")
-        nc.scalar.dma_start(b_rows[:], b.rearrange("(g k) o -> g (k o)", k=H))
+        bias = held.tile([H, len(GATES)], F32, name="bias")
+        with nc.allow_non_contiguous_dma(reason="2.5 KiB of bias, one element to a partition"):
+            nc.scalar.dma_start(bias[:], b.rearrange("(g k) o -> k (g o)", k=H))
 
         window = {}
 
@@ -49,18 +49,16 @@ def tile_sympleagent_kernel(tc, table, ua, ub, b, offs, out):
         for gate in ("fa", "fb"):
             load_window(gate)
 
-        identity = held.tile([len(GATES), len(GATES)], F32, name="identity")
-        masks.make_identity(nc, identity[:])
-        bias_psum = psum.tile([H, len(GATES)], F32, name="bias_psum")
-        nc.tensor.matmul(bias_psum[:], b_rows[:], identity[:], start=True, stop=True)
+        def bias_of(gate):
+            g = GATES.index(gate)
+            return bias[:, g : g + 1]
 
         bias_wide = {}
         for gate in ("i", "u", "o"):
             bias_wide[gate] = held.tile([H, LEAVES], F32, name="bias_wide_" + gate)
-            g = GATES.index(gate)
-            nc.vector.tensor_copy(bias_wide[gate][:], bias_psum[:, g : g + 1].to_broadcast([H, LEAVES]))
-        bias = held.tile([H, len(GATES)], F32, name="bias")
-        nc.vector.tensor_copy(bias[:], bias_psum[:])
+        nc.vector.tensor_copy(bias_wide["i"][:], bias_of("i").to_broadcast([H, LEAVES]))
+        nc.scalar.copy(bias_wide["u"][:], bias_of("u").to_broadcast([H, LEAVES]))
+        nc.scalar.copy(bias_wide["o"][:], bias_of("o").to_broadcast([H, LEAVES]))
 
         leaf_offsets = offsets[:, 0 : LEAVES // 16]
         leaf = {}
@@ -85,7 +83,7 @@ def tile_sympleagent_kernel(tc, table, ua, ub, b, offs, out):
             nc.tensor.matmul(products[:], ua_sb[:, g * H : (g + 1) * H], hl[:, 0:B], start=True, stop=False)
             nc.tensor.matmul(products[:], ub_sb[:, g * H : (g + 1) * H], hl[:, B:LEAVES], start=False, stop=True)
             kids = held.tile([H, B], F32, name="kids_" + gate)
-            nc.scalar.activation(kids[:], products[:], IDENTITY, bias=bias[:, g : g + 1])
+            nc.scalar.activation(kids[:], products[:], IDENTITY, bias=bias_of(gate))
             z = held.tile([H, B], F32, name="z_root_" + gate)
             nc.vector.tensor_tensor(z[:], window[gate][:].indirect(root_offsets), kids[:], ADD)
             root[gate] = held.tile([H, B], F32, name="root_" + gate)

@@ -14,10 +14,21 @@ S = 512
 B = 128
 LEAVES = 2 * B
 N = LEAVES + B
+PER_COLUMN = 16
 GATES = ("i", "fa", "fb", "o", "u")
 FUNC = {"i": SIGMOID, "fa": SIGMOID, "fb": SIGMOID, "o": SIGMOID, "u": TANH}
+HALF = B // 2
+HALVES = (0, 1)
 
 FLOPS = 2 * 2 * H * len(GATES) * H * B
+
+
+def trees_of(half):
+    return slice(half * HALF, (half + 1) * HALF)
+
+
+def leaves_of(tile, half):
+    return tile[:].rearrange("p (side t) -> p side t", t=B)[:, :, trees_of(half)]
 
 
 def tile_sympleagent_kernel(tc, table, ua, ub, b, offs, out):
@@ -26,7 +37,7 @@ def tile_sympleagent_kernel(tc, table, ua, ub, b, offs, out):
         tc.tile_pool(name="held", bufs=1) as held,
         tc.psum_pool(name="psum", bufs=1) as psum,
     ):
-        offsets = held.tile([128, N // 16], U16, name="offsets")
+        offsets = held.tile([H, N // PER_COLUMN], U16, name="offsets")
         nc.sync.dma_start(offsets[:], offs)
 
         bias = held.tile([H, len(GATES)], F32, name="bias")
@@ -56,49 +67,69 @@ def tile_sympleagent_kernel(tc, table, ua, ub, b, offs, out):
         bias_wide = {}
         for gate in ("i", "u", "o"):
             bias_wide[gate] = held.tile([H, LEAVES], F32, name="bias_wide_" + gate)
-        nc.vector.tensor_copy(bias_wide["i"][:], bias_of("i").to_broadcast([H, LEAVES]))
-        nc.scalar.copy(bias_wide["u"][:], bias_of("u").to_broadcast([H, LEAVES]))
-        nc.scalar.copy(bias_wide["o"][:], bias_of("o").to_broadcast([H, LEAVES]))
+            nc.vector.tensor_copy(bias_wide[gate][:], bias_of(gate).to_broadcast([H, LEAVES]))
 
-        leaf_offsets = offsets[:, 0 : LEAVES // 16]
+        leaf_offsets = offsets[:, 0 : LEAVES // PER_COLUMN]
+        z_leaf = {}
         leaf = {}
         for gate in ("i", "u", "o"):
-            z = held.tile([H, LEAVES], F32, name="z_leaf_" + gate)
-            nc.vector.tensor_tensor(z[:], window[gate][:].indirect(leaf_offsets), bias_wide[gate][:], ADD)
+            z_leaf[gate] = held.tile([H, LEAVES], F32, name="z_leaf_" + gate)
+            nc.vector.tensor_tensor(
+                z_leaf[gate][:], window[gate][:].indirect(leaf_offsets), bias_wide[gate][:], ADD
+            )
             leaf[gate] = held.tile([H, LEAVES], F32, name="leaf_" + gate)
-            nc.scalar.activation(leaf[gate][:], z[:], FUNC[gate])
+        nc.scalar.activation(leaf["i"][:], z_leaf["i"][:], FUNC["i"])
+        nc.scalar.activation(leaf["u"][:], z_leaf["u"][:], FUNC["u"])
 
         cl = held.tile([H, LEAVES], F32, name="cl")
-        nc.vector.tensor_tensor(cl[:], leaf["i"][:], leaf["u"][:], MULT)
         tanh_cl = held.tile([H, LEAVES], F32, name="tanh_cl")
-        nc.scalar.activation(tanh_cl[:], cl[:], TANH)
-        hl = held.tile([H, LEAVES], BF16, name="hl")
-        nc.vector.tensor_tensor(hl[:], leaf["o"][:], tanh_cl[:], MULT)
+        for half in HALVES:
+            nc.scalar.activation(leaves_of(leaf["o"], half), leaves_of(z_leaf["o"], half), FUNC["o"])
+            nc.vector.tensor_tensor(leaves_of(cl, half), leaves_of(leaf["i"], half), leaves_of(leaf["u"], half), MULT)
+            nc.scalar.activation(leaves_of(tanh_cl, half), leaves_of(cl, half), TANH)
 
-        root_offsets = offsets[:, LEAVES // 16 : N // 16]
-        root = {}
-        for gate in ("i", "u", "fa", "fb", "o"):
-            g = GATES.index(gate)
-            products = psum.tile([H, B], F32, name="products_" + gate)
-            nc.tensor.matmul(products[:], ua_sb[:, g * H : (g + 1) * H], hl[:, 0:B], start=True, stop=False)
-            nc.tensor.matmul(products[:], ub_sb[:, g * H : (g + 1) * H], hl[:, B:LEAVES], start=False, stop=True)
-            kids = held.tile([H, B], F32, name="kids_" + gate)
-            nc.scalar.activation(kids[:], products[:], IDENTITY, bias=bias_of(gate))
-            z = held.tile([H, B], F32, name="z_root_" + gate)
-            nc.vector.tensor_tensor(z[:], window[gate][:].indirect(root_offsets), kids[:], ADD)
-            root[gate] = held.tile([H, B], F32, name="root_" + gate)
-            nc.scalar.activation(root[gate][:], z[:], FUNC[gate])
+        root_gates = ("i", "u", "fa", "fb", "o")
+        hl = held.tile([H, LEAVES], BF16, name="hl")
+        products = {gate: psum.tile([H, B], F32, name="products_" + gate) for gate in root_gates}
+        kids = {gate: held.tile([H, B], F32, name="kids_" + gate) for gate in root_gates}
+        for half in HALVES:
+            trees = trees_of(half)
+            nc.vector.tensor_tensor(leaves_of(hl, half), leaves_of(leaf["o"], half), leaves_of(tanh_cl, half), MULT)
+            for gate in root_gates:
+                g = GATES.index(gate)
+                left = hl[:, 0:B][:, trees]
+                right = hl[:, B:LEAVES][:, trees]
+                nc.tensor.matmul(products[gate][:, trees], ua_sb[:, g * H : (g + 1) * H], left, start=True, stop=False)
+                nc.tensor.matmul(products[gate][:, trees], ub_sb[:, g * H : (g + 1) * H], right, start=False, stop=True)
+                nc.scalar.activation(kids[gate][:, trees], products[gate][:, trees], IDENTITY, bias=bias_of(gate))
+
+        z_root = {gate: held.tile([H, B], F32, name="z_root_" + gate) for gate in root_gates}
+        root = {gate: held.tile([H, B], F32, name="root_" + gate) for gate in root_gates}
+        for half in HALVES:
+            trees = trees_of(half)
+            first = (LEAVES + half * HALF) // PER_COLUMN
+            root_offsets = offsets[:, first : first + HALF // PER_COLUMN]
+            for gate in root_gates:
+                nc.vector.tensor_tensor(
+                    z_root[gate][:, trees], window[gate][:].indirect(root_offsets), kids[gate][:, trees], ADD
+                )
+                nc.scalar.activation(root[gate][:, trees], z_root[gate][:, trees], FUNC[gate])
 
         cr = held.tile([H, B], F32, name="cr")
         from_left = held.tile([H, B], F32, name="from_left")
         from_right = held.tile([H, B], F32, name="from_right")
-        nc.vector.tensor_tensor(cr[:], root["i"][:], root["u"][:], MULT)
-        nc.vector.tensor_tensor(from_left[:], root["fa"][:], cl[:, 0:B], MULT)
-        nc.vector.tensor_tensor(from_right[:], root["fb"][:], cl[:, B:LEAVES], MULT)
-        nc.vector.tensor_tensor(cr[:], cr[:], from_left[:], ADD)
-        nc.vector.tensor_tensor(cr[:], cr[:], from_right[:], ADD)
         tanh_cr = held.tile([H, B], F32, name="tanh_cr")
-        nc.scalar.activation(tanh_cr[:], cr[:], TANH)
+        for half in HALVES:
+            trees = trees_of(half)
+            nc.vector.tensor_tensor(cr[:, trees], root["i"][:, trees], root["u"][:, trees], MULT)
+            nc.vector.tensor_tensor(from_left[:, trees], root["fa"][:, trees], cl[:, 0:B][:, trees], MULT)
+            nc.vector.tensor_tensor(from_right[:, trees], root["fb"][:, trees], cl[:, B:LEAVES][:, trees], MULT)
+            nc.vector.tensor_tensor(cr[:, trees], cr[:, trees], from_left[:, trees], ADD)
+            nc.vector.tensor_tensor(cr[:, trees], cr[:, trees], from_right[:, trees], ADD)
+            nc.scalar.activation(tanh_cr[:, trees], cr[:, trees], TANH)
+
         hr = held.tile([H, B], F32, name="hr")
-        nc.vector.tensor_tensor(hr[:], root["o"][:], tanh_cr[:], MULT)
-        nc.sync.dma_start(out, hr[:])
+        for half in HALVES:
+            trees = trees_of(half)
+            nc.vector.tensor_tensor(hr[:, trees], root["o"][:, trees], tanh_cr[:, trees], MULT)
+            nc.sync.dma_start(out[:, trees], hr[:, trees])

@@ -35,7 +35,7 @@ def tile_sympleagent_kernel(tc, table, ua, ub, b, offs, out):
     nc = tc.nc
     with (
         tc.tile_pool(name="held", bufs=1) as held,
-        tc.psum_pool(name="psum", bufs=1) as psum,
+        tc.psum_pool(name="psum", bufs=8) as psum,
     ):
         offsets = held.tile([H, N // PER_COLUMN], U16, name="offsets")
         nc.sync.dma_start(offsets[:], offs)
@@ -88,45 +88,61 @@ def tile_sympleagent_kernel(tc, table, ua, ub, b, offs, out):
             nc.vector.tensor_tensor(leaves_of(cl, half), leaves_of(leaf["i"], half), leaves_of(leaf["u"], half), MULT)
             nc.scalar.activation(leaves_of(tanh_cl, half), leaves_of(cl, half), TANH)
 
-        root_gates = ("i", "u", "fa", "fb", "o")
+        cell_gates = ("fa", "fb", "i", "u")
+        root_gates = cell_gates + ("o",)
         hl = held.tile([H, LEAVES], BF16, name="hl")
-        products = {gate: psum.tile([H, B], F32, name="products_" + gate) for gate in root_gates}
         kids = {gate: held.tile([H, B], F32, name="kids_" + gate) for gate in root_gates}
-        for half in HALVES:
-            trees = trees_of(half)
-            nc.vector.tensor_tensor(leaves_of(hl, half), leaves_of(leaf["o"], half), leaves_of(tanh_cl, half), MULT)
-            for gate in root_gates:
-                g = GATES.index(gate)
-                left = hl[:, 0:B][:, trees]
-                right = hl[:, B:LEAVES][:, trees]
-                nc.tensor.matmul(products[gate][:, trees], ua_sb[:, g * H : (g + 1) * H], left, start=True, stop=False)
-                nc.tensor.matmul(products[gate][:, trees], ub_sb[:, g * H : (g + 1) * H], right, start=False, stop=True)
-                nc.scalar.activation(kids[gate][:, trees], products[gate][:, trees], IDENTITY, bias=bias_of(gate))
-
         z_root = {gate: held.tile([H, B], F32, name="z_root_" + gate) for gate in root_gates}
         root = {gate: held.tile([H, B], F32, name="root_" + gate) for gate in root_gates}
-        for half in HALVES:
+
+        def children_term(gate, half):
+            g = GATES.index(gate)
+            trees = trees_of(half)
+            left = hl[:, 0:B][:, trees]
+            right = hl[:, B:LEAVES][:, trees]
+            products = psum.tile([H, HALF], F32, name="products")
+            nc.tensor.matmul(products[:], ua_sb[:, g * H : (g + 1) * H], left, start=True, stop=False)
+            nc.tensor.matmul(products[:], ub_sb[:, g * H : (g + 1) * H], right, start=False, stop=True)
+            nc.scalar.activation(kids[gate][:, trees], products[:], IDENTITY, bias=bias_of(gate))
+
+        def root_gate(gate, half):
             trees = trees_of(half)
             first = (LEAVES + half * HALF) // PER_COLUMN
             root_offsets = offsets[:, first : first + HALF // PER_COLUMN]
-            for gate in root_gates:
-                nc.vector.tensor_tensor(
-                    z_root[gate][:, trees], window[gate][:].indirect(root_offsets), kids[gate][:, trees], ADD
-                )
-                nc.scalar.activation(root[gate][:, trees], z_root[gate][:, trees], FUNC[gate])
+            nc.vector.tensor_tensor(
+                z_root[gate][:, trees], window[gate][:].indirect(root_offsets), kids[gate][:, trees], ADD
+            )
+            nc.scalar.activation(root[gate][:, trees], z_root[gate][:, trees], FUNC[gate])
 
-        cr = held.tile([H, B], F32, name="cr")
+        for half in HALVES:
+            nc.vector.tensor_tensor(leaves_of(hl, half), leaves_of(leaf["o"], half), leaves_of(tanh_cl, half), MULT)
+            for gate in cell_gates:
+                children_term(gate, half)
+        for half in HALVES:
+            children_term("o", half)
+
+        for half in HALVES:
+            for gate in cell_gates:
+                root_gate(gate, half)
+
         from_left = held.tile([H, B], F32, name="from_left")
         from_right = held.tile([H, B], F32, name="from_right")
+        from_children = held.tile([H, B], F32, name="from_children")
+        own = held.tile([H, B], F32, name="own")
+        cr = held.tile([H, B], F32, name="cr")
         tanh_cr = held.tile([H, B], F32, name="tanh_cr")
         for half in HALVES:
             trees = trees_of(half)
-            nc.vector.tensor_tensor(cr[:, trees], root["i"][:, trees], root["u"][:, trees], MULT)
             nc.vector.tensor_tensor(from_left[:, trees], root["fa"][:, trees], cl[:, 0:B][:, trees], MULT)
             nc.vector.tensor_tensor(from_right[:, trees], root["fb"][:, trees], cl[:, B:LEAVES][:, trees], MULT)
-            nc.vector.tensor_tensor(cr[:, trees], cr[:, trees], from_left[:, trees], ADD)
-            nc.vector.tensor_tensor(cr[:, trees], cr[:, trees], from_right[:, trees], ADD)
+            nc.vector.tensor_tensor(from_children[:, trees], from_left[:, trees], from_right[:, trees], ADD)
+        for half in HALVES:
+            trees = trees_of(half)
+            nc.vector.tensor_tensor(own[:, trees], root["i"][:, trees], root["u"][:, trees], MULT)
+            nc.vector.tensor_tensor(cr[:, trees], own[:, trees], from_children[:, trees], ADD)
             nc.scalar.activation(tanh_cr[:, trees], cr[:, trees], TANH)
+        for half in HALVES:
+            root_gate("o", half)
 
         hr = held.tile([H, B], F32, name="hr")
         for half in HALVES:

@@ -71,21 +71,29 @@ def tile_sympleagent_kernel(tc, table, ua, ub, b, offs, out):
 
         leaf_offsets = offsets[:, 0 : LEAVES // PER_COLUMN]
         z_leaf = {}
-        leaf = {}
         for gate in ("i", "u", "o"):
             z_leaf[gate] = held.tile([H, LEAVES], F32, name="z_leaf_" + gate)
             nc.vector.tensor_tensor(
                 z_leaf[gate][:], window[gate][:].indirect(leaf_offsets), bias_wide[gate][:], ADD
             )
-            leaf[gate] = held.tile([H, LEAVES], F32, name="leaf_" + gate)
-        nc.scalar.activation(leaf["i"][:], z_leaf["i"][:], FUNC["i"])
-        nc.scalar.activation(leaf["u"][:], z_leaf["u"][:], FUNC["u"])
+        leaf_i = held.tile([H, LEAVES], F32, name="leaf_i")
+        nc.scalar.activation(leaf_i[:], z_leaf["i"][:], FUNC["i"])
 
+        def by_side(tile):
+            return tile[:].rearrange("p (side t) -> p side t", t=HALF)
+
+        leaf_u = [held.tile([H, 2 * HALF], F32, name="leaf_u_%d" % half) for half in HALVES]
+        for half in HALVES:
+            nc.scalar.activation(by_side(leaf_u[half]), leaves_of(z_leaf["u"], half), FUNC["u"])
+
+        place_of_leaf_o = ("leaf_o_0", "leaf_u_0")
+        leaf_o = []
         cl = held.tile([H, LEAVES], F32, name="cl")
         tanh_cl = held.tile([H, LEAVES], F32, name="tanh_cl")
         for half in HALVES:
-            nc.scalar.activation(leaves_of(leaf["o"], half), leaves_of(z_leaf["o"], half), FUNC["o"])
-            nc.vector.tensor_tensor(leaves_of(cl, half), leaves_of(leaf["i"], half), leaves_of(leaf["u"], half), MULT)
+            leaf_o.append(held.tile([H, 2 * HALF], F32, name="leaf_o_%d" % half, tag=place_of_leaf_o[half]))
+            nc.scalar.activation(by_side(leaf_o[half]), leaves_of(z_leaf["o"], half), FUNC["o"])
+            nc.vector.tensor_tensor(leaves_of(cl, half), leaves_of(leaf_i, half), by_side(leaf_u[half]), MULT)
             nc.scalar.activation(leaves_of(tanh_cl, half), leaves_of(cl, half), TANH)
 
         cell_gates = ("fa", "fb", "i", "u")
@@ -115,7 +123,7 @@ def tile_sympleagent_kernel(tc, table, ua, ub, b, offs, out):
             nc.scalar.activation(root[gate][:, trees], z_root[gate][:, trees], FUNC[gate])
 
         for half in HALVES:
-            nc.vector.tensor_tensor(leaves_of(hl, half), leaves_of(leaf["o"], half), leaves_of(tanh_cl, half), MULT)
+            nc.vector.tensor_tensor(leaves_of(hl, half), by_side(leaf_o[half]), leaves_of(tanh_cl, half), MULT)
             for gate in cell_gates:
                 children_term(gate, half)
         for half in HALVES:

@@ -103,20 +103,17 @@ def tile_sympleagent_kernel(tc, table, ua, ub, b, offs, out):
         z_root = {gate: held.tile([H, B], F32, name="z_root_" + gate) for gate in root_gates}
         root = {gate: held.tile([H, B], F32, name="root_" + gate) for gate in root_gates}
 
-        def children_term(gate, half):
+        def children_term(gate, trees):
             g = GATES.index(gate)
-            trees = trees_of(half)
             left = hl[:, 0:B][:, trees]
             right = hl[:, B:LEAVES][:, trees]
-            products = psum.tile([H, HALF], F32, name="products")
+            products = psum.tile([H, trees.stop - trees.start], F32, name="products")
             nc.tensor.matmul(products[:], ua_sb[:, g * H : (g + 1) * H], left, start=True, stop=False)
             nc.tensor.matmul(products[:], ub_sb[:, g * H : (g + 1) * H], right, start=False, stop=True)
             nc.scalar.activation(kids[gate][:, trees], products[:], IDENTITY, bias=bias_of(gate))
 
-        def root_gate(gate, half):
-            trees = trees_of(half)
-            first = (LEAVES + half * HALF) // PER_COLUMN
-            root_offsets = offsets[:, first : first + HALF // PER_COLUMN]
+        def root_gate(gate, trees):
+            root_offsets = offsets[:, (LEAVES + trees.start) // PER_COLUMN : (LEAVES + trees.stop) // PER_COLUMN]
             nc.vector.tensor_tensor(
                 z_root[gate][:, trees], window[gate][:].indirect(root_offsets), kids[gate][:, trees], ADD
             )
@@ -125,13 +122,13 @@ def tile_sympleagent_kernel(tc, table, ua, ub, b, offs, out):
         for half in HALVES:
             nc.vector.tensor_tensor(leaves_of(hl, half), by_side(leaf_o[half]), leaves_of(tanh_cl, half), MULT)
             for gate in cell_gates:
-                children_term(gate, half)
-        for half in HALVES:
-            children_term("o", half)
+                children_term(gate, trees_of(half))
+        all_trees = slice(0, B)
+        children_term("o", all_trees)
 
         for half in HALVES:
             for gate in cell_gates:
-                root_gate(gate, half)
+                root_gate(gate, trees_of(half))
 
         from_left = held.tile([H, B], F32, name="from_left")
         from_right = held.tile([H, B], F32, name="from_right")
@@ -149,8 +146,7 @@ def tile_sympleagent_kernel(tc, table, ua, ub, b, offs, out):
             nc.vector.tensor_tensor(own[:, trees], root["i"][:, trees], root["u"][:, trees], MULT)
             nc.vector.tensor_tensor(cr[:, trees], own[:, trees], from_children[:, trees], ADD)
             nc.scalar.activation(tanh_cr[:, trees], cr[:, trees], TANH)
-        for half in HALVES:
-            root_gate("o", half)
+        root_gate("o", all_trees)
 
         hr = held.tile([H, B], F32, name="hr")
         for half in HALVES:

@@ -19,6 +19,11 @@ GATES = ("i", "fa", "fb", "o", "u")
 FUNC = {"i": SIGMOID, "fa": SIGMOID, "fb": SIGMOID, "o": SIGMOID, "u": TANH}
 HALF = B // 2
 HALVES = (0, 1)
+PIECE = HALF // 2
+
+
+def pieces_of(half):
+    return [slice(start, start + PIECE) for start in range(half * HALF, (half + 1) * HALF, PIECE)]
 
 FLOPS = 2 * 2 * H * len(GATES) * H * B
 
@@ -27,8 +32,8 @@ def trees_of(half):
     return slice(half * HALF, (half + 1) * HALF)
 
 
-def leaves_of(tile, half):
-    return tile[:].rearrange("p (side t) -> p side t", t=B)[:, :, trees_of(half)]
+def leaves_of(tile, trees):
+    return tile[:].rearrange("p (side t) -> p side t", t=B)[:, :, trees]
 
 
 def tile_sympleagent_kernel(tc, table, ua, ub, b, offs, out):
@@ -79,12 +84,14 @@ def tile_sympleagent_kernel(tc, table, ua, ub, b, offs, out):
         leaf_i = held.tile([H, LEAVES], F32, name="leaf_i")
         nc.scalar.activation(leaf_i[:], z_leaf["i"][:], FUNC["i"])
 
-        def by_side(tile):
-            return tile[:].rearrange("p (side t) -> p side t", t=HALF)
+        def by_side(tile, half, trees):
+            in_half = slice(trees.start - half * HALF, trees.stop - half * HALF)
+            return tile[:].rearrange("p (side t) -> p side t", t=HALF)[:, :, in_half]
 
         leaf_u = [held.tile([H, 2 * HALF], F32, name="leaf_u_%d" % half) for half in HALVES]
         for half in HALVES:
-            nc.scalar.activation(by_side(leaf_u[half]), leaves_of(z_leaf["u"], half), FUNC["u"])
+            for piece in pieces_of(half):
+                nc.scalar.activation(by_side(leaf_u[half], half, piece), leaves_of(z_leaf["u"], piece), FUNC["u"])
 
         place_of_leaf_o = ("leaf_o_0", "leaf_u_0")
         leaf_o = []
@@ -92,9 +99,12 @@ def tile_sympleagent_kernel(tc, table, ua, ub, b, offs, out):
         tanh_cl = held.tile([H, LEAVES], F32, name="tanh_cl")
         for half in HALVES:
             leaf_o.append(held.tile([H, 2 * HALF], F32, name="leaf_o_%d" % half, tag=place_of_leaf_o[half]))
-            nc.scalar.activation(by_side(leaf_o[half]), leaves_of(z_leaf["o"], half), FUNC["o"])
-            nc.vector.tensor_tensor(leaves_of(cl, half), leaves_of(leaf_i, half), by_side(leaf_u[half]), MULT)
-            nc.scalar.activation(leaves_of(tanh_cl, half), leaves_of(cl, half), TANH)
+            trees = trees_of(half)
+            nc.scalar.activation(by_side(leaf_o[half], half, trees), leaves_of(z_leaf["o"], trees), FUNC["o"])
+            for piece in pieces_of(half):
+                u_of_piece = by_side(leaf_u[half], half, piece)
+                nc.vector.tensor_tensor(leaves_of(cl, piece), leaves_of(leaf_i, piece), u_of_piece, MULT)
+                nc.scalar.activation(leaves_of(tanh_cl, piece), leaves_of(cl, piece), TANH)
 
         cell_gates = ("fa", "fb", "i", "u")
         root_gates = cell_gates + ("o",)
@@ -120,7 +130,9 @@ def tile_sympleagent_kernel(tc, table, ua, ub, b, offs, out):
             nc.scalar.activation(root[gate][:, trees], z_root[gate][:, trees], FUNC[gate])
 
         for half in HALVES:
-            nc.vector.tensor_tensor(leaves_of(hl, half), by_side(leaf_o[half]), leaves_of(tanh_cl, half), MULT)
+            for piece in pieces_of(half):
+                o_of_piece = by_side(leaf_o[half], half, piece)
+                nc.vector.tensor_tensor(leaves_of(hl, piece), o_of_piece, leaves_of(tanh_cl, piece), MULT)
             for gate in cell_gates:
                 children_term(gate, trees_of(half))
         all_trees = slice(0, B)

@@ -45,9 +45,19 @@ def tile_sympleagent_kernel(tc, table, ua, ub, b, offs, out):
         offsets = held.tile([H, N // PER_COLUMN], U16, name="offsets")
         nc.sync.dma_start(offsets[:], offs)
 
-        bias = held.tile([H, len(GATES)], F32, name="bias")
-        with nc.allow_non_contiguous_dma(reason="2.5 KiB of bias, one element to a partition"):
-            nc.scalar.dma_start(bias[:], b.rearrange("(g k) o -> k (g o)", k=H))
+        by_gate = b.rearrange("(g k) o -> k (g o)", k=H)
+        bias = {}
+
+        def load_bias(queue, gates):
+            first = GATES.index(gates[0])
+            part = held.tile([H, len(gates)], F32, name="bias_" + "_".join(gates))
+            with nc.allow_non_contiguous_dma(reason="at most 1 KiB of bias, one element to a partition"):
+                queue.dma_start(part[:], by_gate[:, first : first + len(gates)])
+            for column, gate in enumerate(gates):
+                bias[gate] = part[:, column : column + 1]
+
+        load_bias(nc.scalar, ("i",))
+        load_bias(nc.scalar, ("o", "u"))
 
         window = {}
 
@@ -58,21 +68,22 @@ def tile_sympleagent_kernel(tc, table, ua, ub, b, offs, out):
 
         for gate in ("i", "u", "o"):
             load_window(gate)
+        load_bias(nc.sync, ("fa", "fb"))
         ua_sb = held.tile([H, len(GATES) * H], BF16, name="ua_sb")
         ub_sb = held.tile([H, len(GATES) * H], BF16, name="ub_sb")
-        nc.sync.dma_start(ua_sb[:], ua)
         nc.sync.dma_start(ub_sb[:], ub)
+        nc.sync.dma_start(ua_sb[:], ua)
         for gate in ("fa", "fb"):
             load_window(gate)
 
-        def bias_of(gate):
-            g = GATES.index(gate)
-            return bias[:, g : g + 1]
-
-        bias_wide = {}
-        for gate in ("i", "u", "o"):
-            bias_wide[gate] = held.tile([H, LEAVES], F32, name="bias_wide_" + gate)
-            nc.vector.tensor_copy(bias_wide[gate][:], bias_of(gate).to_broadcast([H, LEAVES]))
+        zero = held.tile([H, 1], F32, name="zero")
+        nc.vector.memset(zero[:], 0.0)
+        set_loader = held.tile([H, 1], F32, name="set_loader")
+        nc.scalar.activation(set_loader[:], zero[:], SIGMOID)
+        bias_wide = {gate: held.tile([H, LEAVES], F32, name="bias_wide_" + gate) for gate in ("i", "u", "o")}
+        nc.vector.tensor_copy(bias_wide["i"][:], bias["i"].to_broadcast([H, LEAVES]))
+        for gate in ("u", "o"):
+            nc.scalar.activation(bias_wide[gate][:], bias[gate].to_broadcast([H, LEAVES]), IDENTITY)
 
         leaf_offsets = offsets[:, 0 : LEAVES // PER_COLUMN]
         z_leaf = {}
@@ -111,7 +122,11 @@ def tile_sympleagent_kernel(tc, table, ua, ub, b, offs, out):
         hl = held.tile([H, LEAVES], BF16, name="hl")
         kids = {gate: held.tile([H, B], F32, name="kids_" + gate) for gate in root_gates}
         z_root = {gate: held.tile([H, B], F32, name="z_root_" + gate) for gate in root_gates}
-        root = {gate: held.tile([H, B], F32, name="root_" + gate) for gate in root_gates}
+        root_f = held.tile([H, LEAVES], F32, name="root_f")
+        root = {"fa": root_f[:, 0:B], "fb": root_f[:, B:LEAVES]}
+        for gate in ("i", "u", "o"):
+            root_of_gate = held.tile([H, B], F32, name="root_" + gate)
+            root[gate] = root_of_gate[:]
 
         def children_term(gate, trees):
             g = GATES.index(gate)
@@ -120,7 +135,7 @@ def tile_sympleagent_kernel(tc, table, ua, ub, b, offs, out):
             products = psum.tile([H, trees.stop - trees.start], F32, name="products")
             nc.tensor.matmul(products[:], ua_sb[:, g * H : (g + 1) * H], left, start=True, stop=False)
             nc.tensor.matmul(products[:], ub_sb[:, g * H : (g + 1) * H], right, start=False, stop=True)
-            nc.scalar.activation(kids[gate][:, trees], products[:], IDENTITY, bias=bias_of(gate))
+            nc.scalar.activation(kids[gate][:, trees], products[:], IDENTITY, bias=bias[gate])
 
         def root_gate(gate, trees):
             root_offsets = offsets[:, (LEAVES + trees.start) // PER_COLUMN : (LEAVES + trees.stop) // PER_COLUMN]
@@ -142,16 +157,17 @@ def tile_sympleagent_kernel(tc, table, ua, ub, b, offs, out):
             for gate in cell_gates:
                 root_gate(gate, trees_of(half))
 
-        from_left = held.tile([H, B], F32, name="from_left")
-        from_right = held.tile([H, B], F32, name="from_right")
+        from_each = held.tile([H, LEAVES], F32, name="from_each")
         from_children = held.tile([H, B], F32, name="from_children")
         own = held.tile([H, B], F32, name="own")
         cr = held.tile([H, B], F32, name="cr")
         tanh_cr = held.tile([H, B], F32, name="tanh_cr")
         for half in HALVES:
             trees = trees_of(half)
-            nc.vector.tensor_tensor(from_left[:, trees], root["fa"][:, trees], cl[:, 0:B][:, trees], MULT)
-            nc.vector.tensor_tensor(from_right[:, trees], root["fb"][:, trees], cl[:, B:LEAVES][:, trees], MULT)
+            nc.vector.tensor_tensor(
+                leaves_of(from_each, trees), leaves_of(root_f, trees), leaves_of(cl, trees), MULT
+            )
+            from_left, from_right = from_each[:, 0:B], from_each[:, B:LEAVES]
             nc.vector.tensor_tensor(from_children[:, trees], from_left[:, trees], from_right[:, trees], ADD)
         for half in HALVES:
             trees = trees_of(half)

@@ -7,6 +7,7 @@ ADD = mybir.AluOpType.add
 MULT = mybir.AluOpType.mult
 SIGMOID = mybir.ActivationFunctionType.Sigmoid
 TANH = mybir.ActivationFunctionType.Tanh
+X = mybir.AxisListType.X
 IDENTITY = mybir.ActivationFunctionType.Identity
 
 H = 128
@@ -157,22 +158,18 @@ def tile_sympleagent_kernel(tc, table, ua, ub, b, offs, out):
             for gate in cell_gates:
                 root_gate(gate, trees_of(half))
 
-        from_each = held.tile([H, LEAVES], F32, name="from_each")
-        from_children = held.tile([H, B], F32, name="from_children")
-        own = held.tile([H, B], F32, name="own")
+        terms = held.tile([H, 3 * B], F32, name="terms")
+        by_term = terms[:].rearrange("p (term t) -> p term t", term=3)
+        by_tree = terms[:].rearrange("p (term t) -> p t term", term=3)
         cr = held.tile([H, B], F32, name="cr")
         tanh_cr = held.tile([H, B], F32, name="tanh_cr")
         for half in HALVES:
             trees = trees_of(half)
-            nc.vector.tensor_tensor(
-                leaves_of(from_each, trees), leaves_of(root_f, trees), leaves_of(cl, trees), MULT
-            )
-            from_left, from_right = from_each[:, 0:B], from_each[:, B:LEAVES]
-            nc.vector.tensor_tensor(from_children[:, trees], from_left[:, trees], from_right[:, trees], ADD)
+            nc.vector.tensor_tensor(by_term[:, 0:2, trees], leaves_of(root_f, trees), leaves_of(cl, trees), MULT)
         for half in HALVES:
             trees = trees_of(half)
-            nc.vector.tensor_tensor(own[:, trees], root["i"][:, trees], root["u"][:, trees], MULT)
-            nc.vector.tensor_tensor(cr[:, trees], own[:, trees], from_children[:, trees], ADD)
+            nc.vector.tensor_tensor(by_term[:, 2, trees], root["i"][:, trees], root["u"][:, trees], MULT)
+            nc.vector.tensor_reduce(cr[:, trees], by_tree[:, trees, :], axis=X, op=ADD)
             nc.scalar.activation(tanh_cr[:, trees], cr[:, trees], TANH)
         root_gate("o", all_trees)
 

@@ -19,6 +19,7 @@ PER_COLUMN = 16
 GATES = ("i", "fa", "fb", "o", "u")
 FUNC = {"i": SIGMOID, "fa": SIGMOID, "fb": SIGMOID, "o": SIGMOID, "u": TANH}
 HALF = B // 2
+LAST_PIECE = B + HALF
 HALVES = (0, 1)
 PIECE = HALF // 2
 
@@ -86,13 +87,20 @@ def tile_sympleagent_kernel(tc, table, ua, ub, b, offs, out):
         for gate in ("u", "o"):
             nc.scalar.activation(bias_wide[gate][:], bias[gate].to_broadcast([H, LEAVES]), IDENTITY)
 
-        leaf_offsets = offsets[:, 0 : LEAVES // PER_COLUMN]
-        z_leaf = {}
-        for gate in ("i", "u", "o"):
-            z_leaf[gate] = held.tile([H, LEAVES], F32, name="z_leaf_" + gate)
+        def look_up_leaves(z, gate, first, last):
             nc.vector.tensor_tensor(
-                z_leaf[gate][:], window[gate][:].indirect(leaf_offsets), bias_wide[gate][:], ADD
+                z,
+                window[gate][:].indirect(offsets[:, first // PER_COLUMN : last // PER_COLUMN]),
+                bias_wide[gate][:, first:last],
+                ADD,
             )
+
+        z_leaf = {gate: held.tile([H, LEAVES], F32, name="z_leaf_" + gate) for gate in ("i", "u")}
+        z_leaf["o"] = held.tile([H, LAST_PIECE], F32, name="z_leaf_o")
+        look_up_leaves(z_leaf["i"][:], "i", 0, LEAVES)
+        look_up_leaves(z_leaf["u"][:, 0:LAST_PIECE], "u", 0, LAST_PIECE)
+        look_up_leaves(z_leaf["u"][:, LAST_PIECE:LEAVES], "u", LAST_PIECE, LEAVES)
+        look_up_leaves(z_leaf["o"][:], "o", 0, LAST_PIECE)
         leaf_i = held.tile([H, LEAVES], F32, name="leaf_i")
         nc.scalar.activation(leaf_i[:], z_leaf["i"][:], FUNC["i"])
 
@@ -105,18 +113,22 @@ def tile_sympleagent_kernel(tc, table, ua, ub, b, offs, out):
             for piece in pieces_of(half):
                 nc.scalar.activation(by_side(leaf_u[half], half, piece), leaves_of(z_leaf["u"], piece), FUNC["u"])
 
-        place_of_leaf_o = ("leaf_o_0", "leaf_u_0")
-        leaf_o = []
+        leaf_o = [held.tile([H, 2 * HALF], F32, name="leaf_o_%d" % half) for half in HALVES]
+        left_of_half, right_of_half = slice(0, HALF), slice(HALF, 2 * HALF)
+        nc.scalar.activation(leaf_o[0][:, left_of_half], z_leaf["o"][:, 0:HALF], FUNC["o"])
+        nc.scalar.activation(leaf_o[0][:, right_of_half], z_leaf["o"][:, B:LAST_PIECE], FUNC["o"])
         cl = held.tile([H, LEAVES], F32, name="cl")
         tanh_cl = held.tile([H, LEAVES], F32, name="tanh_cl")
         for half in HALVES:
-            leaf_o.append(held.tile([H, 2 * HALF], F32, name="leaf_o_%d" % half, tag=place_of_leaf_o[half]))
-            trees = trees_of(half)
-            nc.scalar.activation(by_side(leaf_o[half], half, trees), leaves_of(z_leaf["o"], trees), FUNC["o"])
             for piece in pieces_of(half):
                 u_of_piece = by_side(leaf_u[half], half, piece)
                 nc.vector.tensor_tensor(leaves_of(cl, piece), leaves_of(leaf_i, piece), u_of_piece, MULT)
                 nc.scalar.activation(leaves_of(tanh_cl, piece), leaves_of(cl, piece), TANH)
+            if half == 0:
+                z_leaf_o_last = held.tile([H, 2 * HALF], F32, name="z_leaf_o_last", tag="leaf_u_0")
+                look_up_leaves(z_leaf_o_last[:, 0:HALF], "o", LAST_PIECE, LEAVES)
+                nc.scalar.activation(leaf_o[1][:, left_of_half], z_leaf["o"][:, HALF:B], FUNC["o"])
+                nc.scalar.activation(leaf_o[1][:, right_of_half], z_leaf_o_last[:, 0:HALF], FUNC["o"])
 
         cell_gates = ("fa", "fb", "i", "u")
         root_gates = cell_gates + ("o",)

@@ -134,7 +134,11 @@ def tile_sympleagent_kernel(tc, table, ua, ub, b, offs, out):
         root_gates = cell_gates + ("o",)
         hl = held.tile([H, LEAVES], BF16, name="hl")
         kids = {gate: held.tile([H, B], F32, name="kids_" + gate) for gate in root_gates}
-        z_root = {gate: held.tile([H, B], F32, name="z_root_" + gate) for gate in root_gates}
+        z_root_f = held.tile([H, LEAVES], F32, name="z_root_f")
+        z_root = {"fa": z_root_f[:, 0:B], "fb": z_root_f[:, B:LEAVES]}
+        for gate in ("i", "u", "o"):
+            z_of_gate = held.tile([H, B], F32, name="z_root_" + gate)
+            z_root[gate] = z_of_gate[:]
         root_f = held.tile([H, LEAVES], F32, name="root_f")
         root = {"fa": root_f[:, 0:B], "fb": root_f[:, B:LEAVES]}
         for gate in ("i", "u", "o"):
@@ -155,7 +159,10 @@ def tile_sympleagent_kernel(tc, table, ua, ub, b, offs, out):
             nc.vector.tensor_tensor(
                 z_root[gate][:, trees], window[gate][:].indirect(root_offsets), kids[gate][:, trees], ADD
             )
-            nc.scalar.activation(root[gate][:, trees], z_root[gate][:, trees], FUNC[gate])
+            if gate == "fb":
+                nc.scalar.activation(leaves_of(root_f, trees), leaves_of(z_root_f, trees), SIGMOID)
+            elif gate != "fa":
+                nc.scalar.activation(root[gate][:, trees], z_root[gate][:, trees], FUNC[gate])
 
         for half in HALVES:
             for piece in pieces_of(half):

import concourse.mybir as mybir

F32 = mybir.dt.float32
BF16 = mybir.dt.bfloat16
U16 = mybir.dt.uint16
ADD = mybir.AluOpType.add
MULT = mybir.AluOpType.mult
SIGMOID = mybir.ActivationFunctionType.Sigmoid
TANH = mybir.ActivationFunctionType.Tanh
X = mybir.AxisListType.X
IDENTITY = mybir.ActivationFunctionType.Identity

H = 128
S = 512
B = 128
LEAVES = 2 * B
N = LEAVES + B
PER_COLUMN = 16
GATES = ("i", "fa", "fb", "o", "u")
FUNC = {"i": SIGMOID, "fa": SIGMOID, "fb": SIGMOID, "o": SIGMOID, "u": TANH}
HALF = B // 2
LAST_PIECE = B + HALF
HALVES = (0, 1)
PIECE = HALF // 2


def pieces_of(half):
    return [slice(start, start + PIECE) for start in range(half * HALF, (half + 1) * HALF, PIECE)]

FLOPS = 2 * 2 * H * len(GATES) * H * B


def trees_of(half):
    return slice(half * HALF, (half + 1) * HALF)


def leaves_of(tile, trees):
    return tile[:].rearrange("p (side t) -> p side t", t=B)[:, :, trees]


def tile_sympleagent_kernel(tc, table, ua, ub, b, offs, out):
    nc = tc.nc
    with (
        tc.tile_pool(name="held", bufs=1) as held,
        tc.psum_pool(name="psum", bufs=8) as psum,
    ):
        offsets = held.tile([H, N // PER_COLUMN], U16, name="offsets")
        nc.sync.dma_start(offsets[:], offs)

        by_gate = b.rearrange("(g k) o -> k (g o)", k=H)
        bias = {}

        def load_bias(queue, gates):
            first = GATES.index(gates[0])
            part = held.tile([H, len(gates)], F32, name="bias_" + "_".join(gates))
            with nc.allow_non_contiguous_dma(reason="at most 1 KiB of bias, one element to a partition"):
                queue.dma_start(part[:], by_gate[:, first : first + len(gates)])
            for column, gate in enumerate(gates):
                bias[gate] = part[:, column : column + 1]

        load_bias(nc.scalar, ("i",))
        load_bias(nc.scalar, ("o", "u"))

        window = {}

        def load_window(gate):
            g = GATES.index(gate)
            window[gate] = held.tile([H, S], F32, name="window_" + gate)
            nc.sync.dma_start(window[gate][:], table[g * H : (g + 1) * H, :])

        for gate in ("i", "u", "o"):
            load_window(gate)
        load_bias(nc.sync, ("fa", "fb"))
        ua_sb = held.tile([H, len(GATES) * H], BF16, name="ua_sb")
        ub_sb = held.tile([H, len(GATES) * H], BF16, name="ub_sb")
        nc.sync.dma_start(ub_sb[:], ub)
        nc.sync.dma_start(ua_sb[:], ua)
        for gate in ("fa", "fb"):
            load_window(gate)

        zero = held.tile([H, 1], F32, name="zero")
        nc.vector.memset(zero[:], 0.0)
        set_loader = held.tile([H, 1], F32, name="set_loader")
        nc.scalar.activation(set_loader[:], zero[:], SIGMOID)
        bias_wide = {gate: held.tile([H, LEAVES], F32, name="bias_wide_" + gate) for gate in ("i", "u", "o")}
        nc.vector.tensor_copy(bias_wide["i"][:], bias["i"].to_broadcast([H, LEAVES]))
        for gate in ("u", "o"):
            nc.scalar.activation(bias_wide[gate][:], bias[gate].to_broadcast([H, LEAVES]), IDENTITY)

        def look_up_leaves(z, gate, first, last):
            nc.vector.tensor_tensor(
                z,
                window[gate][:].indirect(offsets[:, first // PER_COLUMN : last // PER_COLUMN]),
                bias_wide[gate][:, first:last],
                ADD,
            )

        z_leaf = {gate: held.tile([H, LEAVES], F32, name="z_leaf_" + gate) for gate in ("i", "u")}
        z_leaf["o"] = held.tile([H, LAST_PIECE], F32, name="z_leaf_o")
        look_up_leaves(z_leaf["i"][:], "i", 0, LEAVES)
        look_up_leaves(z_leaf["u"][:, 0:LAST_PIECE], "u", 0, LAST_PIECE)
        look_up_leaves(z_leaf["u"][:, LAST_PIECE:LEAVES], "u", LAST_PIECE, LEAVES)
        look_up_leaves(z_leaf["o"][:], "o", 0, LAST_PIECE)
        leaf_i = held.tile([H, LEAVES], F32, name="leaf_i")
        nc.scalar.activation(leaf_i[:], z_leaf["i"][:], FUNC["i"])

        def by_side(tile, half, trees):
            in_half = slice(trees.start - half * HALF, trees.stop - half * HALF)
            return tile[:].rearrange("p (side t) -> p side t", t=HALF)[:, :, in_half]

        leaf_u = [held.tile([H, 2 * HALF], F32, name="leaf_u_%d" % half) for half in HALVES]
        for half in HALVES:
            for piece in pieces_of(half):
                nc.scalar.activation(by_side(leaf_u[half], half, piece), leaves_of(z_leaf["u"], piece), FUNC["u"])

        leaf_o = [held.tile([H, 2 * HALF], F32, name="leaf_o_%d" % half) for half in HALVES]
        left_of_half, right_of_half = slice(0, HALF), slice(HALF, 2 * HALF)
        nc.scalar.activation(leaf_o[0][:, left_of_half], z_leaf["o"][:, 0:HALF], FUNC["o"])
        nc.scalar.activation(leaf_o[0][:, right_of_half], z_leaf["o"][:, B:LAST_PIECE], FUNC["o"])
        cl = held.tile([H, LEAVES], F32, name="cl")
        tanh_cl = held.tile([H, LEAVES], F32, name="tanh_cl")
        for half in HALVES:
            for piece in pieces_of(half):
                u_of_piece = by_side(leaf_u[half], half, piece)
                nc.vector.tensor_tensor(leaves_of(cl, piece), leaves_of(leaf_i, piece), u_of_piece, MULT)
                nc.scalar.activation(leaves_of(tanh_cl, piece), leaves_of(cl, piece), TANH)
            if half == 0:
                z_leaf_o_last = held.tile([H, 2 * HALF], F32, name="z_leaf_o_last", tag="leaf_u_0")
                look_up_leaves(z_leaf_o_last[:, 0:HALF], "o", LAST_PIECE, LEAVES)
                nc.scalar.activation(leaf_o[1][:, left_of_half], z_leaf["o"][:, HALF:B], FUNC["o"])
                nc.scalar.activation(leaf_o[1][:, right_of_half], z_leaf_o_last[:, 0:HALF], FUNC["o"])

        cell_gates = ("fa", "fb", "i", "u")
        root_gates = cell_gates + ("o",)
        hl = held.tile([H, LEAVES], BF16, name="hl")
        kids = {gate: held.tile([H, B], F32, name="kids_" + gate) for gate in root_gates}
        z_root_f = held.tile([H, LEAVES], F32, name="z_root_f")
        z_root = {"fa": z_root_f[:, 0:B], "fb": z_root_f[:, B:LEAVES]}
        for gate in ("i", "u", "o"):
            z_of_gate = held.tile([H, B], F32, name="z_root_" + gate)
            z_root[gate] = z_of_gate[:]
        root_f = held.tile([H, LEAVES], F32, name="root_f")
        root = {"fa": root_f[:, 0:B], "fb": root_f[:, B:LEAVES]}
        for gate in ("i", "u", "o"):
            root_of_gate = held.tile([H, B], F32, name="root_" + gate)
            root[gate] = root_of_gate[:]

        def children_term(gate, trees):
            g = GATES.index(gate)
            left = hl[:, 0:B][:, trees]
            right = hl[:, B:LEAVES][:, trees]
            products = psum.tile([H, trees.stop - trees.start], F32, name="products")
            nc.tensor.matmul(products[:], ua_sb[:, g * H : (g + 1) * H], left, start=True, stop=False)
            nc.tensor.matmul(products[:], ub_sb[:, g * H : (g + 1) * H], right, start=False, stop=True)
            nc.scalar.activation(kids[gate][:, trees], products[:], IDENTITY, bias=bias[gate])

        def root_gate(gate, trees):
            root_offsets = offsets[:, (LEAVES + trees.start) // PER_COLUMN : (LEAVES + trees.stop) // PER_COLUMN]
            nc.vector.tensor_tensor(
                z_root[gate][:, trees], window[gate][:].indirect(root_offsets), kids[gate][:, trees], ADD
            )
            if gate == "fb":
                nc.scalar.activation(leaves_of(root_f, trees), leaves_of(z_root_f, trees), SIGMOID)
            elif gate != "fa":
                nc.scalar.activation(root[gate][:, trees], z_root[gate][:, trees], FUNC[gate])

        for half in HALVES:
            for piece in pieces_of(half):
                o_of_piece = by_side(leaf_o[half], half, piece)
                nc.vector.tensor_tensor(leaves_of(hl, piece), o_of_piece, leaves_of(tanh_cl, piece), MULT)
            for gate in cell_gates:
                children_term(gate, trees_of(half))
        all_trees = slice(0, B)
        children_term("o", all_trees)

        for half in HALVES:
            for gate in cell_gates:
                root_gate(gate, trees_of(half))

        terms = held.tile([H, 3 * B], F32, name="terms")
        by_term = terms[:].rearrange("p (term t) -> p term t", term=3)
        by_tree = terms[:].rearrange("p (term t) -> p t term", term=3)
        cr = held.tile([H, B], F32, name="cr")
        tanh_cr = held.tile([H, B], F32, name="tanh_cr")
        for half in HALVES:
            trees = trees_of(half)
            nc.vector.tensor_tensor(by_term[:, 0:2, trees], leaves_of(root_f, trees), leaves_of(cl, trees), MULT)
        for half in HALVES:
            trees = trees_of(half)
            nc.vector.tensor_tensor(by_term[:, 2, trees], root["i"][:, trees], root["u"][:, trees], MULT)
            nc.vector.tensor_reduce(cr[:, trees], by_tree[:, trees, :], axis=X, op=ADD)
            nc.scalar.activation(tanh_cr[:, trees], cr[:, trees], TANH)
        root_gate("o", all_trees)

        hr = held.tile([H, B], F32, name="hr")
        for half in HALVES:
            trees = trees_of(half)
            nc.vector.tensor_tensor(hr[:, trees], root["o"][:, trees], tanh_cr[:, trees], MULT)
            nc.sync.dma_start(out[:, trees], hr[:, trees])
